import numpy as np
import ml_dtypes


def mxq(x, axis, fmt="e4m3"):
    dtype, down = {"e4m3": (ml_dtypes.float8_e4m3fn, 7), "e5m2": (ml_dtypes.float8_e5m2, 14)}[fmt]
    v = np.moveaxis(np.asarray(x, np.float32).astype(ml_dtypes.bfloat16).astype(np.float64), axis, -1)
    blocks = v.reshape(v.shape[:-1] + (-1, 32))
    amax = np.abs(blocks).max(-1, keepdims=True)
    byte = np.maximum(np.where(amax > 0, np.frexp(amax)[1] - 1 + 127, 0) - down, 1)
    scale = np.exp2(byte - 127.0)
    codes = (blocks / scale).astype(np.float32).astype(dtype).astype(np.float64)
    return np.moveaxis((codes * scale).reshape(v.shape), -1, axis)


WIDE = False


def mx_kscale(k):
    if not WIDE:
        return np.ones(k)
    levels = np.array([10, -10, 5, -5, 0])
    if k % 512:
        return np.exp2(np.random.permutation(np.resize(levels, k // 32))).repeat(32)
    a = np.empty((k // 512, 16))
    for p in range(k // 512):
        a[p, :8] = np.random.permutation(np.resize(levels, 8))
        for g in range(8):
            far = levels[np.abs(levels - a[p, g]) >= 10]
            a[p, g + 8] = far[np.random.randint(len(far))]
    return np.exp2(a.ravel()).repeat(32)


BF16 = ml_dtypes.bfloat16


def bf(x):
    return np.asarray(x, np.float32).astype(BF16)


def f64(x):
    return np.asarray(x).astype(np.float64)


L, B, D, F, TC = 8, 4096, 512, 1024, 4
EPS = 1e-5
NT = 100
ERF_C = 1.0 / np.cumprod(2.0 * np.arange(NT) + 1.0)


def erf(v):
    a = np.minimum(np.abs(v), 6.0)
    q = 2.0 * a * a
    acc = np.full_like(q, ERF_C[-1])
    for c in ERF_C[-2::-1]:
        acc = acc * q + c
    return np.sign(v) * (2.0 / np.sqrt(np.pi)) * a * np.exp(-a * a) * acc


def gelu(v):
    return 0.5 * v * (1.0 + erf(v / np.sqrt(2.0)))


def layer_norm(x, g, b):
    m = x.mean(-1, keepdims=True)
    v = ((x - m) ** 2).mean(-1, keepdims=True)
    return (x - m) / np.sqrt(v + EPS) * g + b


def draw0():
    s, t = mx_kscale(D), mx_kscale(F)
    return {"z": bf(np.random.standard_normal((B, D)) * s),
            "W1": bf(np.random.standard_normal((D, F)) / np.sqrt(D) / s[:, None]),
            "b1": bf(np.random.standard_normal(F) * 0.3),
            "g1": bf((1.0 + 0.1 * np.random.standard_normal(F)) * t),
            "be1": bf(0.1 * np.random.standard_normal(F) * t),
            "W2": bf(np.random.standard_normal((F, D)) / np.sqrt(F) / t[:, None]),
            "b2": bf(np.random.standard_normal(D) * 0.3),
            "g2": bf(1.0 + 0.1 * np.random.standard_normal(D)),
            "be2": bf(0.1 * np.random.standard_normal(D))}


def core(z, W1, b1, g1, be1, W2, b2, g2, be2):
    h = gelu((mxq(f64(z), 1, "e4m3") @ mxq(f64(W1), 0, "e4m3")) + f64(b1))
    h = layer_norm(h, f64(g1), f64(be1))
    return layer_norm((mxq(h, 1, "e4m3") @ mxq(f64(W2), 0, "e4m3")) + f64(b2), f64(g2), f64(be2))


def e4m3fn_bytes(y):
    return np.clip(np.asarray(y, np.float64), -448.0, 448.0).astype(np.float32).astype(ml_dtypes.float8_e4m3fn).view(np.uint8)


def e4m3fn_values(b):
    return np.asarray(b, np.uint8).view(ml_dtypes.float8_e4m3fn).astype(np.float64)


def setup_inputs():
    d = draw0()
    x0 = np.asarray(d['z']).astype(np.float64)
    s = (np.max(np.abs(x0), axis=(0,), keepdims=True) / 448.0).astype(np.float32)
    out = {}
    for k, v in d.items():
        if k == 'z':
            out['z_bytes'] = e4m3fn_bytes(x0 / s.astype(np.float64))
            out['z_scale'] = s
        else:
            out[k] = v
    return out


def reference(z_bytes, z_scale, W1, b1, g1, be1, W2, b2, g2, be2):
    return core(e4m3fn_values(z_bytes) * z_scale.astype(np.float64), W1, b1, g1, be1, W2, b2, g2, be2)

from contextlib import ExitStack

import concourse.mybir as mybir
from concourse.masks import make_identity

TOKENS, D, HID = 4096, 512, 1024
FLOPS = 2 * TOKENS * D * HID * 2
EPS = 1e-5

F32 = mybir.dt.float32
BF16 = mybir.dt.bfloat16
U32 = mybir.dt.uint32
U8 = mybir.dt.uint8
FP8 = mybir.dt.float8_e4m3fn
FP8X4 = mybir.dt.float8_e4m3fn_x4
ACT = mybir.ActivationFunctionType
ALU = mybir.AluOpType

P = 128
TILES = 4
GROUP = P * TILES
GROUPS = TOKENS // GROUP
NT = TOKENS // P
CHUNKS = HID // P
HALF = GROUP // 2

MANUAL = True
ARR_G = ()
AFF_V = ()
AFF_V_LAST = ()
ORDER = [
    ("h_quantize", 6),
    ("out_mean", 11),
    ("h_norm", 1),
    ("h_transpose", 0),
    ("back_transpose", 4),
    ("h_stats", 0),
    ("load_z", -19),
    ("affine", 4),
    ("z_transpose", -8),
    ("out_tail", 11),
    ("product", -11),
    ("arrange", 5),
    ("out_square", 11),
    ("out_last", 12),
    ("h_rstd", 0),
    ("out_rstd", 11),
    ("z_exit", -8),
    ("w1_quantize", -6),
    ("z_quantize", -6),
    ("hidden_mm", -4),
    ("out_mm", 9),
    ("w2_quantize", 3),
    ("hidden_gelu", -4),
    ("w1_arrange", -8),
    ("w2_arrange", -3),
    ("out_bias", 9),
]


def tile_emaaggregator_pa_t_kernel(tc, z_bytes, z_scale, W1, b1, g1, be1, W2, b2, g2, be2, out):
    nc = tc.nc
    z_view = z_bytes.rearrange("(x p j) k -> x p j k", p=P, j=TILES)
    out_view = out.rearrange("(x p j) d -> x p j d", p=P, j=TILES)
    w1_view = W1.rearrange("(p j) n -> p j n", j=4)
    w2_view = W2.rearrange("(g p j) n -> g p j n", g=2, j=4)

    with ExitStack() as ctx:
        keep = ctx.enter_context(tc.tile_pool(name="keep", bufs=1))
        work = ctx.enter_context(tc.tile_pool(name="work", bufs=2))
        psum = ctx.enter_context(tc.psum_pool(name="psum", bufs=1))
        if MANUAL:
            ctx.enter_context(tc.manual_schedule())

        t = {}

        def load_z(x):
            raw = work.tile([P, TILES, D], U8, name="zraw", tag="zraw", bufs=3, align_bytes=64)
            nc.sync.dma_start(out=raw[:], in_=z_view[x])
            t["zraw", x] = raw

        warm = keep.tile([P, 1], F32, name="warm")
        nc.vector.memset(warm[:], 0.0)
        warm_out = keep.tile([P, 1], F32, name="warm_out")
        nc.scalar.activation(out=warm_out[:], in_=warm[:], func=ACT.Gelu)

        load_z(0)
        scale_b = keep.tile([P, D], F32, name="scale_b")
        nc.sync.dma_start(out=scale_b[:], in_=z_scale.rearrange("o k -> (o k)").partition_broadcast(P))
        w1_raw = []
        for g in range(2):
            raw = keep.tile([P, 4, 512], BF16, name="w1_raw%d" % g)
            nc.sync.dma_start(out=raw[:], in_=w1_view[:, :, 512 * g : 512 * (g + 1)])
            w1_raw.append(raw)

        def load_channels(vec, nm):
            raw = keep.tile([P, 2, 4], BF16, name=nm)
            nc.sync.dma_start(out=raw[:], in_=vec.rearrange("(g p t) -> p g t", g=2, t=4))
            return raw

        b1_raw = load_channels(b1, "b1_raw")
        load_z(1)
        g1_raw = load_channels(g1, "g1_raw")
        be1_raw = load_channels(be1, "be1_raw")
        w2_raw = []
        for g in range(2):
            raw = keep.tile([P, 4, D], BF16, name="w2_raw%d" % g)
            nc.sync.dma_start(out=raw[:], in_=w2_view[g])
            w2_raw.append(raw)

        def load_row(vec, nm):
            row = keep.tile([P, D], BF16, name=nm)
            nc.sync.dma_start(out=row[:], in_=vec.partition_broadcast(P))
            return row

        b2_b = load_row(b2, "b2_b")
        g2_b = load_row(g2, "g2_b")
        be2_b = load_row(be2, "be2_b")

        ident = keep.tile([P, P], F32, name="ident")
        make_identity(nc, ident[:])
        nhalf = keep.tile([P, 1], F32, name="nhalf")
        nc.gpsimd.memset(nhalf[:], -0.5)

        def widen(raw, nm):
            f = keep.tile([P, CHUNKS], F32, name=nm)
            nc.gpsimd.tensor_copy(out=f[:], in_=raw[:].rearrange("p g t -> p (g t)"))
            return f

        b1_f = widen(b1_raw, "b1_f")
        g1_f = widen(g1_raw, "g1_f")
        be1_f = widen(be1_raw, "be1_f")

        w1_codes = keep.tile([P, HID], U32, name="w1_codes", align_bytes=64)
        w1_scales = keep.tile([P, HID], U8, name="w1_scales", align_bytes=64)
        w2_codes = keep.tile([P, 2, D], U32, name="w2_codes", align_bytes=64)
        w2_scales = keep.tile([P, 2, D], U8, name="w2_scales", align_bytes=64)
        wg = []
        for i in range(4):
            w = keep.tile([P, 2048], BF16, name="wg%d" % i, align_bytes=64)
            wg.append(w)

        def w1_arrange(g):
            o = wg[g][:].rearrange("p (t m j) -> p t m j", t=4, j=4)
            i = w1_raw[g][:].rearrange("p j (m t) -> p t m j", t=4)
            if g == 0:
                nc.vector.tensor_copy(out=o, in_=i)
            else:
                nc.scalar.copy(out=o, in_=i)

        def w1_quantize(g):
            c = slice(512 * g, 512 * (g + 1))
            nc.vector.quantize_mx(out=w1_codes[:, c].bitcast(FP8X4), scales=w1_scales[:, c], in_=wg[g][:])

        def w2_arrange(g):
            nc.vector.tensor_copy(
                out=wg[2 + g][:].rearrange("p (n j) -> p n j", j=4), in_=w2_raw[g][:].rearrange("p j n -> p n j")
            )

        def w2_quantize(g):
            nc.vector.quantize_mx(out=w2_codes[:, g, :].bitcast(FP8X4), scales=w2_scales[:, g, :], in_=wg[2 + g][:])

        def product(n):
            x, j = divmod(n, TILES)
            if j == 0:
                t["zb", x] = work.tile([P, TILES, D], BF16, name="zb", tag="zb")
            nc.vector.tensor_tensor(
                out=t["zb", x][:, j, :], in0=t["zraw", x][:, j, :].bitcast(FP8), in1=scale_b[:], op=ALU.mult
            )

        def z_transpose(q):
            x, h = divmod(q, 2)
            zt = psum.tile([P, 2, 2, P], F32, name="zt", tag="io", bufs=1)
            for a in range(2):
                words = t["zb", x][:, 2 * h + a, :].bitcast(F32)
                for u in range(2):
                    nc.tensor.transpose(zt[:, a, u, :], words[:, u:256:2], ident[:])
            if h == 0:
                t["zg", x] = work.tile([P, 2048], BF16, name="zg", tag="zg", align_bytes=64)
            t["zt", q] = zt

        def z_exit(q):
            x, h = divmod(q, 2)
            zt = t["zt", q]
            nc.scalar.copy(
                out=t["zg", x][:, 1024 * h : 1024 * (h + 1)].bitcast(F32).rearrange("p (a r u) -> p a r u", a=2, u=2),
                in_=zt[:].rearrange("p a u r -> p a r u"),
            )

        def z_quantize(x):
            codes = work.tile([P, GROUP], U32, name="zcodes", tag="zcodes", align_bytes=64)
            scales = work.tile([P, GROUP], U8, name="zscales", tag="zscales", align_bytes=64)
            nc.vector.quantize_mx(out=codes[:].bitcast(FP8X4), scales=scales[:], in_=t["zg", x][:])
            t["zq", x] = (codes, scales)

        def hidden_mm(k):
            x, c = divmod(k, CHUNKS)
            ps = psum.tile([P, GROUP], F32, name="sx", tag="sx", bufs=3)
            codes, scales = t["zq", x]
            cc = slice(P * c, P * (c + 1))
            nc.tensor.matmul_mx(
                out=ps[:],
                lhsT=w1_codes[:, cc].bitcast(FP8X4),
                lhsT_scale=w1_scales[:, cc],
                rhs=codes[:].bitcast(FP8X4),
                rhs_scale=scales[:],
                start=True,
                stop=True,
            )
            t["hps", x, c] = ps

        def hidden_gelu(k):
            x, c = divmod(k, CHUNKS)
            if c == 0:
                t["hT", x] = work.tile([P, CHUNKS, GROUP], F32, name="hT", tag="hT")
            nc.scalar.activation(
                out=t["hT", x][:, c, :], in_=t["hps", x, c][:], func=ACT.Gelu, bias=b1_f[:, c : c + 1]
            )

        def h_transpose(n):
            x, j = divmod(n, TILES)
            for g in range(2):
                ps = psum.tile([P, 4, P], F32, name="ht", tag="ht", bufs=4)
                for i in range(4):
                    nc.tensor.transpose(ps[:, i, :], t["hT", x][:, 4 * g + i, P * j : P * (j + 1)], ident[:])
                t["ht", n, g] = ps

        def h_stats(n):
            st = work.tile([P, 2, 6], F32, name="st", tag="st", bufs=3)
            for g in range(2):
                nc.vector.bn_stats(out=st[:, g, :], in_=t["ht", n, g][:].rearrange("p i r -> p (i r)"))
            mv = work.tile([P, 2], F32, name="mv", tag="mv", bufs=3)
            nc.vector.bn_aggr(out=mv[:], in_=st[:].rearrange("p g s -> p (g s)"))
            t["mv", n] = mv

        def h_rstd(n):
            mv = t["mv", n]
            ve = work.tile([P, 1], F32, name="ve", tag="ve", bufs=3)
            nc.gpsimd.tensor_scalar(out=ve[:], in0=mv[:, 1:2], scalar1=1.0, scalar2=EPS, op0=ALU.mult, op1=ALU.add)
            r = work.tile([P, 1], F32, name="r", tag="r", bufs=3)
            nc.gpsimd.tensor_tensor(out=r[:], in0=ve[:], in1=nhalf[:], op=ALU.pow)
            nmr = work.tile([P, 1], F32, name="nmr", tag="nmr", bufs=3)
            nc.gpsimd.tensor_scalar(out=nmr[:], in0=mv[:, 0:1], scalar1=r[:], scalar2=-1.0, op0=ALU.mult, op1=ALU.mult)
            t["ln1", n] = (r, nmr)

        def h_norm(n):
            r, nmr = t["ln1", n]
            hn = work.tile([P, HID], F32, name="hn", tag="hn", bufs=9)
            for g in range(2):
                nc.scalar.activation(
                    out=hn[:, 512 * g : 512 * (g + 1)],
                    in_=t["ht", n, g][:].rearrange("p i r -> p (i r)"),
                    func=ACT.Identity,
                    scale=r[:],
                    bias=nmr[:],
                )
            t["hn", n] = hn

        def back_transpose(k):
            x, c = divmod(k, CHUNKS)
            ps = psum.tile([P, GROUP], F32, name="sx", tag="sx", bufs=3)
            for j in range(TILES):
                nc.tensor.transpose(
                    ps[:, P * j : P * (j + 1)], t["hn", TILES * x + j][:, P * c : P * (c + 1)], ident[:]
                )
            t["bps", x, c] = ps

        def affine(k):
            x, c = divmod(k, CHUNKS)
            g, i = divmod(c, 4)
            if i == 0:
                t["hq", x, g] = work.tile([P, 4, GROUP], BF16, name="hq", tag="hq", bufs=4)
            if (c in AFF_V) or (x == GROUPS - 1 and c in AFF_V_LAST):
                nc.vector.tensor_scalar(
                    out=t["hq", x, g][:, i, :],
                    in0=t["bps", x, c][:],
                    scalar1=g1_f[:, c : c + 1],
                    scalar2=be1_f[:, c : c + 1],
                    op0=ALU.mult,
                    op1=ALU.add,
                )
            else:
                nc.scalar.activation(
                    out=t["hq", x, g][:, i, :],
                    in_=t["bps", x, c][:],
                    func=ACT.Identity,
                    scale=g1_f[:, c : c + 1],
                    bias=be1_f[:, c : c + 1],
                )

        def arrange(k):
            x, e = divmod(k, 4)
            g, h = divmod(e, 2)
            hg = work.tile([P, HALF, 4], BF16, name="hg", tag="hg", bufs=4, align_bytes=64)
            src = t["hq", x, g][:, :, HALF * h : HALF * (h + 1)].rearrange("p t n -> p n t")
            if e in ARR_G:
                nc.gpsimd.tensor_scalar(out=hg[:], in0=src, scalar1=1.0, scalar2=0.0, op0=ALU.mult, op1=ALU.add)
            else:
                nc.vector.tensor_copy(out=hg[:], in_=src)
            t["hg", x, g, h] = hg

        def h_quantize(k):
            x, e = divmod(k, 4)
            g, h = divmod(e, 2)
            if g == 0 and h == 0:
                codes = work.tile([P, 2, GROUP], U32, name="hcodes", tag="hcodes", align_bytes=64)
                scales = work.tile([P, 2, GROUP], U8, name="hscales", tag="hscales", align_bytes=64)
                t["hc", x] = (codes, scales)
            codes, scales = t["hc", x]
            c = slice(HALF * h, HALF * (h + 1))
            nc.vector.quantize_mx(
                out=codes[:, g, c].bitcast(FP8X4),
                scales=scales[:, g, c],
                in_=t["hg", x, g, h][:].rearrange("p n t -> p (n t)"),
            )

        def out_mm(n):
            x, j = divmod(n, TILES)
            codes, scales = t["hc", x]
            ps = psum.tile([P, D], F32, name="ops", tag="io", bufs=1)
            r = slice(P * j, P * (j + 1))
            for g in range(2):
                nc.tensor.matmul_mx(
                    out=ps[:],
                    lhsT=codes[:, g, r].bitcast(FP8X4),
                    lhsT_scale=scales[:, g, r],
                    rhs=w2_codes[:, g, :].bitcast(FP8X4),
                    rhs_scale=w2_scales[:, g, :],
                    start=(g == 0),
                    stop=(g == 1),
                )
            t["ops", n] = ps

        def out_bias(n):
            y = work.tile([P, D], F32, name="y", tag="y", bufs=4)
            s1 = work.tile([P, 1], F32, name="s1", tag="s1", bufs=3)
            nc.vector.scalar_tensor_tensor(
                out=y[:], in0=t["ops", n][:], scalar=1.0, in1=b2_b[:], op0=ALU.mult, op1=ALU.add, accum_out=s1[:]
            )
            t["y", n] = y
            t["s1", n] = s1

        def out_mean(n):
            s1 = t["s1", n]
            nm = work.tile([P, 1], F32, name="nm", tag="nm", bufs=4)
            nc.gpsimd.tensor_scalar(out=nm[:], in0=s1[:], scalar1=-1.0 / D, scalar2=0.0, op0=ALU.mult, op1=ALU.add)
            t["nm", n] = nm

        def out_square(n):
            y, nm = t["y", n], t["nm", n]
            sq = work.tile([P, D], BF16, name="sq", tag="sq", bufs=2)
            ss = work.tile([P, 1], F32, name="ss", tag="ss", bufs=3)
            nc.scalar.activation(out=sq[:], in_=y[:], func=ACT.Square, bias=nm[:], accum_out=ss[:])
            t["ss", n] = ss

        def out_rstd(n):
            ss = t["ss", n]
            ve = work.tile([P, 1], F32, name="ve2", tag="ve2", bufs=3)
            nc.gpsimd.tensor_scalar(out=ve[:], in0=ss[:], scalar1=1.0 / D, scalar2=EPS, op0=ALU.mult, op1=ALU.add)
            r = work.tile([P, 1], F32, name="r2", tag="r2", bufs=3)
            nc.gpsimd.tensor_tensor(out=r[:], in0=ve[:], in1=nhalf[:], op=ALU.pow)
            t["r2", n] = r

        def out_tail(n):
            y, nm = t["y", n], t["nm", n]
            u = work.tile([P, D], F32, name="u", tag="u", bufs=3)
            nc.vector.scalar_tensor_tensor(
                out=u[:], in0=y[:], scalar=nm[:], in1=g2_b[:], op0=ALU.add, op1=ALU.mult
            )
            t["u", n] = u

        def out_last(n):
            x, j = divmod(n, TILES)
            o = work.tile([P, D], F32, name="o", tag="o", bufs=4)
            nc.vector.scalar_tensor_tensor(
                out=o[:], in0=t["u", n][:], scalar=t["r2", n][:], in1=be2_b[:], op0=ALU.mult, op1=ALU.add
            )
            nc.sync.dma_start(out=out_view[x][:, j, :], in_=o[:])

        stages = {
            "load_z": (load_z, 0.25, GROUPS),
            "product": (product, 1, NT),
            "z_transpose": (z_transpose, 0.5, 2 * GROUPS),
            "z_exit": (z_exit, 0.5, 2 * GROUPS),
            "z_quantize": (z_quantize, 0.25, GROUPS),
            "hidden_mm": (hidden_mm, 2, 8 * GROUPS),
            "hidden_gelu": (hidden_gelu, 2, 8 * GROUPS),
            "h_transpose": (h_transpose, 1, NT),
            "h_stats": (h_stats, 1, NT),
            "h_rstd": (h_rstd, 1, NT),
            "h_norm": (h_norm, 1, NT),
            "back_transpose": (back_transpose, 2, 8 * GROUPS),
            "affine": (affine, 2, 8 * GROUPS),
            "arrange": (arrange, 1, 4 * GROUPS),
            "h_quantize": (h_quantize, 1, 4 * GROUPS),
            "out_mm": (out_mm, 1, NT),
            "out_bias": (out_bias, 1, NT),
            "out_mean": (out_mean, 1, NT),
            "out_square": (out_square, 1, NT),
            "out_rstd": (out_rstd, 1, NT),
            "out_tail": (out_tail, 1, NT),
            "out_last": (out_last, 1, NT),
            "w1_arrange": (w1_arrange, 2, 2),
            "w1_quantize": (w1_quantize, 2, 2),
            "w2_arrange": (w2_arrange, 1, 2),
            "w2_quantize": (w2_quantize, 1, 2),
        }
        for s in range(-14, NT + 20):
            for nm, first in ORDER:
                fn, rate, count = stages[nm]
                if rate >= 1:
                    for i in range(rate):
                        k = rate * (s - first) + i
                        if 0 <= k < count:
                            fn(k)
                else:
                    every = int(1 / rate)
                    k, rem = divmod(s - first, every)
                    if rem == 0 and 0 <= k < count and not (nm == "load_z" and k < 2):
                        fn(k)
